import numpy as np
import ml_dtypes


def mxq(x, axis, fmt="e4m3"):
    dtype, down = {"e4m3": (ml_dtypes.float8_e4m3fn, 7), "e5m2": (ml_dtypes.float8_e5m2, 14)}[fmt]
    v = np.moveaxis(np.asarray(x, np.float32).astype(ml_dtypes.bfloat16).astype(np.float64), axis, -1)
    blocks = v.reshape(v.shape[:-1] + (-1, 32))
    amax = np.abs(blocks).max(-1, keepdims=True)
    byte = np.maximum(np.where(amax > 0, np.frexp(amax)[1] - 1 + 127, 0) - down, 1)
    scale = np.exp2(byte - 127.0)
    codes = (blocks / scale).astype(np.float32).astype(dtype).astype(np.float64)
    return np.moveaxis((codes * scale).reshape(v.shape), -1, axis)


WIDE = False


def mx_kscale(k):
    if not WIDE:
        return np.ones(k)
    levels = np.array([10, -10, 5, -5, 0])
    a = np.random.permutation(np.resize(levels, k // 512 * 4)).reshape(k // 512, 4)
    idx = np.arange(k)
    return np.exp2(a[idx // 512, idx % 128 // 32])


BF16 = ml_dtypes.bfloat16


def bf(x):
    return np.asarray(x, np.float32).astype(BF16)


def f64(x):
    return np.asarray(x).astype(np.float64)


E2M1 = np.array([0.0, 0.5, 1.0, 1.5, 2.0, 3.0, 4.0, 6.0, -0.0, -0.5, -1.0, -1.5, -2.0, -3.0, -4.0, -6.0])


def pack_weight(w, fmt):
    k, n = w.shape
    w = f64(bf(w)).reshape(k // 32, 32, n)
    amax = np.abs(w).max(1)
    if fmt == "e4m3":
        byte = np.frexp(amax)[1] - 1 + 127 - 7
    else:
        mant, ex = np.frexp(amax / 6.0)
        byte = np.where(mant > 0.5, ex, ex - 1) + 127
    byte = np.clip(np.where(amax > 0, byte, 1), 1, 254)
    scaled = (w * np.exp2(127.0 - byte)[:, None, :]).reshape(k, n).astype(np.float32)
    by_word = np.ascontiguousarray(scaled.reshape(k // 512, 128, 4, n).transpose(0, 1, 3, 2))
    if fmt == "e4m3":
        words = by_word.astype(ml_dtypes.float8_e4m3fn).view(np.uint8)
    else:
        c = by_word.astype(ml_dtypes.float4_e2m1fn).view(np.uint8) & 0xF
        words = c[..., 0::2] | (c[..., 1::2] << 4)
    return np.ascontiguousarray(words), np.ascontiguousarray(byte.astype(np.uint8).reshape(k // 512, 16, n))


def unpack_weight(words, scales, fmt):
    g, p, n, _ = words.shape
    if fmt == "e4m3":
        vals = np.ascontiguousarray(words).view(ml_dtypes.float8_e4m3fn).astype(np.float64)
    else:
        nib = np.empty((g, p, n, 4), np.uint8)
        nib[..., 0::2] = words & 0xF
        nib[..., 1::2] = words >> 4
        vals = E2M1[nib]
    vals = vals * np.repeat(np.exp2(scales.astype(np.float64) - 127.0), 8, axis=1)[..., None]
    return vals.transpose(0, 1, 3, 2).reshape(g * 512, n)

def pack4(w):
    words, scales = pack_weight(w, "e2m1")
    return words.reshape(words.shape[0], 128, -1), scales


def unpack4(words, scales):
    return unpack_weight(words.reshape(words.shape[0], 128, -1, 2), scales, "e2m1")


IN_C, OUT_C, N, ND = 512, 1024, 512, 2


def sigmoid(v):
    return 1.0 / (1.0 + np.exp(-v))


def setup_inputs():
    s, t = mx_kscale(IN_C), mx_kscale(OUT_C)
    rn = np.random.standard_normal
    x = bf(rn((IN_C, N)) * s[:, None])
    h_prev_dim0 = bf(rn((OUT_C, N)) * t[:, None])
    h_prev_dim1 = bf(rn((OUT_C, N)) * t[:, None])
    ct0 = bf(rn((OUT_C, N)) * 0.65)
    ct1 = bf(rn((OUT_C, N)) * 0.65)
    w_io = rn((OUT_C, IN_C)) * 0.7 / np.sqrt(IN_C) / s[None, :]
    w_ho = rn((OUT_C, OUT_C)) * 0.7 / np.sqrt(OUT_C) / t[None, :]
    b_o = bf(rn((OUT_C, 1)) * 0.5)
    weighted_sum = bf(0.4 + 0.5 * np.random.random(ND))
    w_io_words, w_io_scales = pack4(np.ascontiguousarray(w_io.T))
    w_ho_words, w_ho_scales = pack4(np.ascontiguousarray(w_ho.T))
    return {"x": x,
            "h_prev_dim0": h_prev_dim0,
            "h_prev_dim1": h_prev_dim1,
            "ct0": ct0,
            "ct1": ct1,
            "w_io_words": w_io_words,
            "w_io_scales": w_io_scales,
            "w_ho_words": w_ho_words,
            "w_ho_scales": w_ho_scales,
            "b_o": b_o,
            "weighted_sum": weighted_sum}


def reference(x, h_prev_dim0, h_prev_dim1, ct0, ct1, w_io_words, w_io_scales, w_ho_words, w_ho_scales, b_o, weighted_sum):
    xo = unpack4(w_io_words, w_io_scales).T @ mxq(f64(x), 0, "e4m3")
    who = unpack4(w_ho_words, w_ho_scales).T
    ws = f64(weighted_sum)

    def hidden(h_prev, c):
        o = sigmoid(xo + (who @ mxq(f64(h_prev), 0, "e4m3")) + f64(b_o))
        return o * np.tanh(f64(c))

    ht0 = hidden(h_prev_dim0, ct0)
    ht1 = hidden(h_prev_dim1, ct1)
    return ht0 * ws[0] + ht1 * ws[1]

@@ -1,0 +1,172 @@
+from contextlib import ExitStack
+
+import concourse.mybir as mybir
+from concourse.masks import make_identity
+
+BF16 = mybir.dt.bfloat16
+F32 = mybir.dt.float32
+I32 = mybir.dt.int32
+U8 = mybir.dt.uint8
+U32 = mybir.dt.uint32
+FP8X4 = mybir.dt.float8_e4m3fn_x4
+FP4X4 = mybir.dt.float4_e2m1fn_x4
+ACT = mybir.ActivationFunctionType
+ALU = mybir.AluOpType
+
+P = 128
+PACK = 4
+K_PASS = P * PACK
+IN_C, OUT_C, POSITIONS, DIRECTIONS = 512, 1024, 512, 2
+H_PASSES = OUT_C // K_PASS
+W_PASSES = 1 + H_PASSES
+CHUNKS = 1 + DIRECTIONS * H_PASSES
+X_CHUNK = 0
+M_TILES = OUT_C // P
+CT_HALF = M_TILES // 2
+RUN = 4
+VECTOR_POSITIONS = 336
+
+FLOPS = 2 * OUT_C * POSITIONS * (IN_C + DIRECTIONS * OUT_C)
+
+
+def h_chunk(d, g):
+    return 1 + d * H_PASSES + g
+
+
+def tile_mdlstmcellweights_pb_kernel(
+    tc, x, h_prev_dim0, h_prev_dim1, ct0, ct1,
+    w_io_words, w_io_scales, w_ho_words, w_ho_scales, b_o, weighted_sum, out,
+):
+    nc = tc.nc
+    h_prev = [h_prev_dim0, h_prev_dim1]
+    cell = [ct0, ct1]
+    with ExitStack() as ctx:
+        keep = ctx.enter_context(tc.tile_pool(name="keep", bufs=1))
+        work = ctx.enter_context(tc.tile_pool(name="work", bufs=4))
+        psum = ctx.enter_context(tc.psum_pool(name="psum", bufs=8))
+
+        w_words = keep.tile([P, W_PASSES, 2 * OUT_C], U8, align_bytes=64)
+        w_planes = keep.tile([P, W_PASSES, OUT_C], U8, align_bytes=64)
+        raw = keep.tile([P, CHUNKS, PACK, POSITIONS], BF16)
+        grouped = keep.tile([P, CHUNKS, POSITIONS, PACK], BF16, align_bytes=64)
+        a_words = keep.tile([P, CHUNKS, POSITIONS], U32, align_bytes=64)
+        a_planes = keep.tile([P, CHUNKS, POSITIONS], U8, align_bytes=64)
+        cell_sb = keep.tile([P, DIRECTIONS, M_TILES, POSITIONS], BF16)
+        tanh_c = keep.tile([P, DIRECTIONS, M_TILES, POSITIONS], F32)
+        total = keep.tile([P, M_TILES, POSITIONS], F32)
+
+        nc.vector.memset(w_planes[:].rearrange("p g n -> p (g n)").bitcast(I32), 0)
+        warm = keep.tile([P, 1], F32)
+        nc.vector.memset(warm[:], 0.0)
+        nc.scalar.activation(out=warm[:], in_=warm[:], func=ACT.Sigmoid)
+
+        def load_chunk(c, rows):
+            nc.sync.dma_start(out=raw[:, c], in_=rows.rearrange("(p j) w -> p j w", j=PACK))
+
+        def load_h(d):
+            for g in range(H_PASSES):
+                load_chunk(h_chunk(d, g), h_prev[d][g * K_PASS:(g + 1) * K_PASS, :])
+
+        def load_cell(d):
+            for m0 in range(0, M_TILES, CT_HALF):
+                nc.sync.dma_start(
+                    out=cell_sb[:, d, m0:m0 + CT_HALF, :],
+                    in_=cell[d][m0 * P:(m0 + CT_HALF) * P, :].rearrange("(m p) w -> p m w", p=P),
+                )
+
+        load_chunk(X_CHUNK, x)
+        nc.sync.dma_start(out=w_words[:, 0, :].bitcast(I32), in_=w_io_words[0].bitcast(I32))
+        for r in range(4):
+            nc.sync.dma_start(
+                out=w_planes[r:P:32, 0, :].bitcast(I32),
+                in_=w_io_scales[0].rearrange("(q r) n -> r q n", r=4)[r].bitcast(I32),
+            )
+        load_h(0)
+        nc.sync.dma_start(
+            out=w_words[:, 1:W_PASSES, :].bitcast(I32),
+            in_=w_ho_words.rearrange("g p b -> p g b").bitcast(I32),
+        )
+        for r in range(4):
+            nc.sync.dma_start(
+                out=w_planes[r:P:32, 1:W_PASSES, :].bitcast(I32),
+                in_=w_ho_scales.rearrange("g (q r) n -> r q g n", r=4)[r].bitcast(I32),
+            )
+        load_cell(0)
+        load_h(1)
+        load_cell(1)
+
+        identity = keep.tile([P, P], BF16)
+        make_identity(nc, identity[:])
+        bias_rows = keep.tile([P, P], BF16)
+        nc.gpsimd.memset(bias_rows[:], 0.0)
+        nc.gpsimd.dma_start(out=bias_rows[0:M_TILES, :], in_=b_o.rearrange("(m p) o -> m (p o)", p=P))
+        bias_cols = psum.tile([P, P], BF16, tag="acc")
+        nc.tensor.transpose(bias_cols[:], bias_rows[:], identity[:])
+        bias = keep.tile([P, M_TILES], F32)
+        nc.vector.tensor_copy(out=bias[:], in_=bias_cols[:, 0:M_TILES])
+        mix_bf = keep.tile([P, DIRECTIONS], BF16)
+        nc.gpsimd.dma_start(out=mix_bf[:], in_=weighted_sum.partition_broadcast(P))
+        mix = keep.tile([P, DIRECTIONS], F32)
+        nc.vector.tensor_copy(out=mix[:], in_=mix_bf[:])
+
+        def regroup(c, copy, lo, hi):
+            copy(
+                out=grouped[:, c, lo:hi, :].rearrange("p (c i) j -> p c j i", i=RUN),
+                in_=raw[:, c, :, lo:hi].rearrange("p j (c i) -> p c j i", i=RUN),
+            )
+
+        def quantise(c):
+            nc.vector.quantize_mx(
+                out=a_words[:, c, :].bitcast(FP8X4),
+                scales=a_planes[:, c, :],
+                in_=grouped[:, c].rearrange("p w j -> p (w j)"),
+            )
+
+        def mx_pass(acc, m, w_pass, c, start, stop):
+            nc.tensor.matmul_mx(
+                out=acc[:],
+                lhsT=w_words[:, w_pass, 2 * P * m:2 * P * (m + 1)].bitcast(FP4X4),
+                lhsT_scale=w_planes[:, w_pass, P * m:P * (m + 1)],
+                rhs=a_words[:, c, :].bitcast(FP8X4),
+                rhs_scale=a_planes[:, c, :],
+                start=start,
+                stop=stop,
+            )
+
+        def h_passes(acc, d, m):
+            for g in range(H_PASSES):
+                mx_pass(acc, m, 1 + g, h_chunk(d, g), start=False, stop=(g == H_PASSES - 1))
+
+        def gate_times_tanh(acc, d, m, dest):
+            nc.scalar.activation(out=tanh_c[:, d, m, :], in_=cell_sb[:, d, m, :], func=ACT.Tanh)
+            gate = work.tile([P, POSITIONS], F32)
+            nc.scalar.activation(out=gate[:], in_=acc[:], func=ACT.Sigmoid, bias=bias[:, m:m + 1])
+            nc.vector.scalar_tensor_tensor(
+                out=dest, in0=gate[:], scalar=mix[:, d:d + 1], in1=tanh_c[:, d, m, :],
+                op0=ALU.mult, op1=ALU.mult,
+            )
+
+        for c in [X_CHUNK, h_chunk(0, 0), h_chunk(0, 1)]:
+            regroup(c, nc.vector.tensor_copy, 0, VECTOR_POSITIONS)
+            regroup(c, nc.scalar.copy, VECTOR_POSITIONS, POSITIONS)
+            quantise(c)
+        acc0 = []
+        for m in range(M_TILES):
+            acc = psum.tile([P, POSITIONS], F32, tag="acc")
+            mx_pass(acc, m, 0, X_CHUNK, start=True, stop=False)
+            acc0.append(acc)
+        for m in range(M_TILES):
+            h_passes(acc0[m], 0, m)
+            gate_times_tanh(acc0[m], 0, m, total[:, m, :])
+
+        for g in range(H_PASSES):
+            regroup(h_chunk(1, g), nc.vector.tensor_copy, 0, POSITIONS)
+            quantise(h_chunk(1, g))
+        for m in range(M_TILES):
+            acc = psum.tile([P, POSITIONS], F32, tag="acc")
+            mx_pass(acc, m, 0, X_CHUNK, start=True, stop=False)
+            h_passes(acc, 1, m)
+            share = work.tile([P, POSITIONS], F32)
+            gate_times_tanh(acc, 1, m, share[:])
+            nc.vector.tensor_add(out=total[:, m, :], in0=total[:, m, :], in1=share[:])
+            nc.sync.dma_start(out=out[m * P:(m + 1) * P, :], in_=total[:, m, :])

@@ -42,8 +42,8 @@ def tile_mdlstmcellweights_pb_kernel(
     cell = [ct0, ct1]
     with ExitStack() as ctx:
         keep = ctx.enter_context(tc.tile_pool(name="keep", bufs=1))
-        work = ctx.enter_context(tc.tile_pool(name="work", bufs=4))
         psum = ctx.enter_context(tc.psum_pool(name="psum", bufs=8))
+        ctx.enter_context(tc.manual_schedule())
 
         w_words = keep.tile([P, W_PASSES, 2 * OUT_C], U8, align_bytes=64)
         w_planes = keep.tile([P, W_PASSES, OUT_C], U8, align_bytes=64)
@@ -53,35 +53,44 @@ def tile_mdlstmcellweights_pb_kernel(
         a_planes = keep.tile([P, CHUNKS, POSITIONS], U8, align_bytes=64)
         cell_sb = keep.tile([P, DIRECTIONS, M_TILES, POSITIONS], BF16)
         tanh_c = keep.tile([P, DIRECTIONS, M_TILES, POSITIONS], F32)
-        total = keep.tile([P, M_TILES, POSITIONS], F32)
+        gate = keep.tile([P, DIRECTIONS, M_TILES, POSITIONS], F32)
+        share = keep.tile([P, DIRECTIONS, M_TILES, POSITIONS], F32)
 
         nc.vector.memset(w_planes[:].rearrange("p g n -> p (g n)").bitcast(I32), 0)
         warm = keep.tile([P, 1], F32)
         nc.vector.memset(warm[:], 0.0)
         nc.scalar.activation(out=warm[:], in_=warm[:], func=ACT.Sigmoid)
+        bias_rows = keep.tile([P, P], BF16)
+        nc.gpsimd.memset(bias_rows[:], 0.0)
+        identity = keep.tile([P, P], BF16)
+        make_identity(nc, identity[:])
 
         def load_chunk(c, rows):
             nc.sync.dma_start(out=raw[:, c], in_=rows.rearrange("(p j) w -> p j w", j=PACK))
 
-        def load_h(d):
-            for g in range(H_PASSES):
-                load_chunk(h_chunk(d, g), h_prev[d][g * K_PASS:(g + 1) * K_PASS, :])
+        def load_h(d, g):
+            load_chunk(h_chunk(d, g), h_prev[d][g * K_PASS:(g + 1) * K_PASS, :])
 
-        def load_cell(d):
-            for m0 in range(0, M_TILES, CT_HALF):
-                nc.sync.dma_start(
-                    out=cell_sb[:, d, m0:m0 + CT_HALF, :],
-                    in_=cell[d][m0 * P:(m0 + CT_HALF) * P, :].rearrange("(m p) w -> p m w", p=P),
-                )
+        def load_cell(d, half):
+            m0 = half * CT_HALF
+            nc.sync.dma_start(
+                out=cell_sb[:, d, m0:m0 + CT_HALF, :],
+                in_=cell[d][m0 * P:(m0 + CT_HALF) * P, :].rearrange("(m p) w -> p m w", p=P),
+            )
 
         load_chunk(X_CHUNK, x)
+        nc.sync.dma_start(out=bias_rows[0:M_TILES, :], in_=b_o.rearrange("(m p) o -> m (p o)", p=P))
+        mix_bf = keep.tile([P, DIRECTIONS], BF16)
+        nc.sync.dma_start(out=mix_bf[:], in_=weighted_sum.partition_broadcast(P))
         nc.sync.dma_start(out=w_words[:, 0, :].bitcast(I32), in_=w_io_words[0].bitcast(I32))
         for r in range(4):
             nc.sync.dma_start(
                 out=w_planes[r:P:32, 0, :].bitcast(I32),
                 in_=w_io_scales[0].rearrange("(q r) n -> r q n", r=4)[r].bitcast(I32),
             )
-        load_h(0)
+        load_h(0, 0)
+        load_h(0, 1)
+        load_cell(0, 0)
         nc.sync.dma_start(
             out=w_words[:, 1:W_PASSES, :].bitcast(I32),
             in_=w_ho_words.rearrange("g p b -> p g b").bitcast(I32),
@@ -91,29 +100,21 @@ def tile_mdlstmcellweights_pb_kernel(
                 out=w_planes[r:P:32, 1:W_PASSES, :].bitcast(I32),
                 in_=w_ho_scales.rearrange("g (q r) n -> r q g n", r=4)[r].bitcast(I32),
             )
-        load_cell(0)
-        load_h(1)
-        load_cell(1)
-
-        identity = keep.tile([P, P], BF16)
-        make_identity(nc, identity[:])
-        bias_rows = keep.tile([P, P], BF16)
-        nc.gpsimd.memset(bias_rows[:], 0.0)
-        nc.gpsimd.dma_start(out=bias_rows[0:M_TILES, :], in_=b_o.rearrange("(m p) o -> m (p o)", p=P))
-        bias_cols = psum.tile([P, P], BF16, tag="acc")
-        nc.tensor.transpose(bias_cols[:], bias_rows[:], identity[:])
-        bias = keep.tile([P, M_TILES], F32)
-        nc.vector.tensor_copy(out=bias[:], in_=bias_cols[:, 0:M_TILES])
-        mix_bf = keep.tile([P, DIRECTIONS], BF16)
-        nc.gpsimd.dma_start(out=mix_bf[:], in_=weighted_sum.partition_broadcast(P))
-        mix = keep.tile([P, DIRECTIONS], F32)
-        nc.vector.tensor_copy(out=mix[:], in_=mix_bf[:])
+        load_h(1, 0)
+        load_h(1, 1)
+        load_cell(0, 1)
+        load_cell(1, 0)
+        load_cell(1, 1)
 
         def regroup(c, copy, lo, hi):
             copy(
                 out=grouped[:, c, lo:hi, :].rearrange("p (c i) j -> p c j i", i=RUN),
                 in_=raw[:, c, :, lo:hi].rearrange("p j (c i) -> p c j i", i=RUN),
             )
+
+        def regroup_shared(c):
+            regroup(c, nc.vector.tensor_copy, 0, VECTOR_POSITIONS)
+            regroup(c, nc.scalar.copy, VECTOR_POSITIONS, POSITIONS)
 
         def quantise(c):
             nc.vector.quantize_mx(
@@ -133,40 +134,84 @@ def tile_mdlstmcellweights_pb_kernel(
                 stop=stop,
             )
 
+        def x_pass(acc, m):
+            mx_pass(acc, m, 0, X_CHUNK, start=True, stop=False)
+
         def h_passes(acc, d, m):
             for g in range(H_PASSES):
                 mx_pass(acc, m, 1 + g, h_chunk(d, g), start=False, stop=(g == H_PASSES - 1))
 
-        def gate_times_tanh(acc, d, m, dest):
+        def tanh(d, m):
             nc.scalar.activation(out=tanh_c[:, d, m, :], in_=cell_sb[:, d, m, :], func=ACT.Tanh)
-            gate = work.tile([P, POSITIONS], F32)
-            nc.scalar.activation(out=gate[:], in_=acc[:], func=ACT.Sigmoid, bias=bias[:, m:m + 1])
+
+        def sigmoid(acc, d, m):
+            nc.scalar.activation(out=gate[:, d, m, :], in_=acc[:], func=ACT.Sigmoid, bias=bias[:, m:m + 1])
+
+        def product(d, m):
             nc.vector.scalar_tensor_tensor(
-                out=dest, in0=gate[:], scalar=mix[:, d:d + 1], in1=tanh_c[:, d, m, :],
+                out=share[:, d, m, :], in0=gate[:, d, m, :], scalar=mix[:, d:d + 1], in1=tanh_c[:, d, m, :],
                 op0=ALU.mult, op1=ALU.mult,
             )
 
-        for c in [X_CHUNK, h_chunk(0, 0), h_chunk(0, 1)]:
-            regroup(c, nc.vector.tensor_copy, 0, VECTOR_POSITIONS)
-            regroup(c, nc.scalar.copy, VECTOR_POSITIONS, POSITIONS)
-            quantise(c)
-        acc0 = []
-        for m in range(M_TILES):
-            acc = psum.tile([P, POSITIONS], F32, tag="acc")
-            mx_pass(acc, m, 0, X_CHUNK, start=True, stop=False)
-            acc0.append(acc)
-        for m in range(M_TILES):
-            h_passes(acc0[m], 0, m)
-            gate_times_tanh(acc0[m], 0, m, total[:, m, :])
+        def add_and_store(m):
+            nc.vector.tensor_add(out=share[:, 0, m, :], in0=share[:, 0, m, :], in1=share[:, 1, m, :])
+            nc.sync.dma_start(out=out[m * P:(m + 1) * P, :], in_=share[:, 0, m, :])
 
-        for g in range(H_PASSES):
-            regroup(h_chunk(1, g), nc.vector.tensor_copy, 0, POSITIONS)
-            quantise(h_chunk(1, g))
+        bias_cols = psum.tile([P, P], BF16, tag="acc")
+        nc.tensor.transpose(bias_cols[:], bias_rows[:], identity[:])
+        regroup_shared(X_CHUNK)
+        quantise(X_CHUNK)
+        acc0 = []
+        for m in range(M_TILES - 1):
+            acc = psum.tile([P, POSITIONS], F32, tag="acc")
+            x_pass(acc, m)
+            acc0.append(acc)
+        regroup_shared(h_chunk(0, 0))
+        regroup_shared(h_chunk(0, 1))
+        quantise(h_chunk(0, 0))
+        quantise(h_chunk(0, 1))
+        bias = keep.tile([P, M_TILES], F32)
+        nc.vector.tensor_copy(out=bias[:], in_=bias_cols[:, 0:M_TILES])
+        mix = keep.tile([P, DIRECTIONS], F32)
+        nc.vector.tensor_copy(out=mix[:], in_=mix_bf[:])
+        for m in range(3):
+            tanh(0, m)
+        for m in range(M_TILES - 1):
+            h_passes(acc0[m], 0, m)
+        acc = psum.tile([P, POSITIONS], F32, tag="acc")
+        x_pass(acc, M_TILES - 1)
+        acc0.append(acc)
+        h_passes(acc, 0, M_TILES - 1)
+
+        regroup(h_chunk(1, 0), nc.vector.tensor_copy, 0, POSITIONS)
+        sigmoid(acc0[0], 0, 0)
+        product(0, 0)
+        regroup(h_chunk(1, 1), nc.vector.tensor_copy, 0, POSITIONS)
+        quantise(h_chunk(1, 0))
+        tanh(0, 3)
+        sigmoid(acc0[1], 0, 1)
+        product(0, 1)
+        quantise(h_chunk(1, 1))
+        for m in (2, 3):
+            sigmoid(acc0[m], 0, m)
+            product(0, m)
+        for m in range(4, M_TILES):
+            tanh(0, m)
+            sigmoid(acc0[m], 0, m)
+            product(0, m)
+
+        acc1 = []
         for m in range(M_TILES):
             acc = psum.tile([P, POSITIONS], F32, tag="acc")
-            mx_pass(acc, m, 0, X_CHUNK, start=True, stop=False)
+            x_pass(acc, m)
             h_passes(acc, 1, m)
-            share = work.tile([P, POSITIONS], F32)
-            gate_times_tanh(acc, 1, m, share[:])
-            nc.vector.tensor_add(out=total[:, m, :], in0=total[:, m, :], in1=share[:])
-            nc.sync.dma_start(out=out[m * P:(m + 1) * P, :], in_=total[:, m, :])
+            acc1.append(acc)
+        tanh(1, 0)
+        for m in range(M_TILES):
+            sigmoid(acc1[m], 1, m)
+            if m + 1 < M_TILES:
+                tanh(1, m + 1)
+            product(1, m)
+            if m > 0:
+                add_and_store(m - 1)
+        add_and_store(M_TILES - 1)

@@ -62,6 +62,9 @@ def tile_mdlstmcellweights_pb_kernel(
         nc.scalar.activation(out=warm[:], in_=warm[:], func=ACT.Sigmoid)
         bias_rows = keep.tile([P, P], BF16)
         nc.gpsimd.memset(bias_rows[:], 0.0)
+        nc.gpsimd.dma_start(out=bias_rows[0:M_TILES, :], in_=b_o.rearrange("(m p) o -> m (p o)", p=P))
+        mix_bf = keep.tile([P, DIRECTIONS], BF16)
+        nc.gpsimd.dma_start(out=mix_bf[:], in_=weighted_sum.partition_broadcast(P))
         identity = keep.tile([P, P], BF16)
         make_identity(nc, identity[:])
 
@@ -79,16 +82,13 @@ def tile_mdlstmcellweights_pb_kernel(
             )
 
         load_chunk(X_CHUNK, x)
-        nc.sync.dma_start(out=bias_rows[0:M_TILES, :], in_=b_o.rearrange("(m p) o -> m (p o)", p=P))
-        mix_bf = keep.tile([P, DIRECTIONS], BF16)
-        nc.sync.dma_start(out=mix_bf[:], in_=weighted_sum.partition_broadcast(P))
+        load_h(0, 0)
         nc.sync.dma_start(out=w_words[:, 0, :].bitcast(I32), in_=w_io_words[0].bitcast(I32))
         for r in range(4):
             nc.sync.dma_start(
                 out=w_planes[r:P:32, 0, :].bitcast(I32),
                 in_=w_io_scales[0].rearrange("(q r) n -> r q n", r=4)[r].bitcast(I32),
             )
-        load_h(0, 0)
         load_h(0, 1)
         load_cell(0, 0)
         nc.sync.dma_start(
@@ -107,10 +107,7 @@ def tile_mdlstmcellweights_pb_kernel(
         load_cell(1, 1)
 
         def regroup(c, copy, lo, hi):
-            copy(
-                out=grouped[:, c, lo:hi, :].rearrange("p (c i) j -> p c j i", i=RUN),
-                in_=raw[:, c, :, lo:hi].rearrange("p j (c i) -> p c j i", i=RUN),
-            )
+            copy(out=grouped[:, c, lo:hi, :], in_=raw[:, c, :, lo:hi].rearrange("p j w -> p w j"))
 
         def regroup_shared(c):
             regroup(c, nc.vector.tensor_copy, 0, VECTOR_POSITIONS)

@@ -25,6 +25,7 @@ M_TILES = OUT_C // P
 CT_HALF = M_TILES // 2
 RUN = 4
 VECTOR_POSITIONS = 336
+HALF = POSITIONS // 2
 
 FLOPS = 2 * OUT_C * POSITIONS * (IN_C + DIRECTIONS * OUT_C)
 
@@ -138,21 +139,25 @@ def tile_mdlstmcellweights_pb_kernel(
             for g in range(H_PASSES):
                 mx_pass(acc, m, 1 + g, h_chunk(d, g), start=False, stop=(g == H_PASSES - 1))
 
-        def tanh(d, m):
-            nc.scalar.activation(out=tanh_c[:, d, m, :], in_=cell_sb[:, d, m, :], func=ACT.Tanh)
+        def tanh(d, m, tiles=2):
+            nc.scalar.activation(
+                out=tanh_c[:, d, m:m + tiles, :], in_=cell_sb[:, d, m:m + tiles, :], func=ACT.Tanh
+            )
 
         def sigmoid(acc, d, m):
             nc.scalar.activation(out=gate[:, d, m, :], in_=acc[:], func=ACT.Sigmoid, bias=bias[:, m:m + 1])
 
-        def product(d, m):
+        def product(d, m, lo=0, hi=POSITIONS):
             nc.vector.scalar_tensor_tensor(
-                out=share[:, d, m, :], in0=gate[:, d, m, :], scalar=mix[:, d:d + 1], in1=tanh_c[:, d, m, :],
-                op0=ALU.mult, op1=ALU.mult,
+                out=share[:, d, m, lo:hi], in0=gate[:, d, m, lo:hi], scalar=mix[:, d:d + 1],
+                in1=tanh_c[:, d, m, lo:hi], op0=ALU.mult, op1=ALU.mult,
             )
 
-        def add_and_store(m):
-            nc.vector.tensor_add(out=share[:, 0, m, :], in0=share[:, 0, m, :], in1=share[:, 1, m, :])
-            nc.sync.dma_start(out=out[m * P:(m + 1) * P, :], in_=share[:, 0, m, :])
+        def add_and_store(m, lo=0, hi=POSITIONS):
+            nc.vector.tensor_add(
+                out=share[:, 0, m, lo:hi], in0=share[:, 0, m, lo:hi], in1=share[:, 1, m, lo:hi]
+            )
+            nc.sync.dma_start(out=out[m * P:(m + 1) * P, lo:hi], in_=share[:, 0, m, lo:hi])
 
         bias_cols = psum.tile([P, P], BF16, tag="acc")
         nc.tensor.transpose(bias_cols[:], bias_rows[:], identity[:])
@@ -171,8 +176,8 @@ def tile_mdlstmcellweights_pb_kernel(
         nc.vector.tensor_copy(out=bias[:], in_=bias_cols[:, 0:M_TILES])
         mix = keep.tile([P, DIRECTIONS], F32)
         nc.vector.tensor_copy(out=mix[:], in_=mix_bf[:])
-        for m in range(3):
-            tanh(0, m)
+        tanh(0, 0)
+        tanh(0, 2)
         for m in range(M_TILES - 1):
             h_passes(acc0[m], 0, m)
         acc = psum.tile([P, POSITIONS], F32, tag="acc")
@@ -185,7 +190,6 @@ def tile_mdlstmcellweights_pb_kernel(
         product(0, 0)
         regroup(h_chunk(1, 1), nc.vector.tensor_copy, 0, POSITIONS)
         quantise(h_chunk(1, 0))
-        tanh(0, 3)
         sigmoid(acc0[1], 0, 1)
         product(0, 1)
         quantise(h_chunk(1, 1))
@@ -193,7 +197,8 @@ def tile_mdlstmcellweights_pb_kernel(
             sigmoid(acc0[m], 0, m)
             product(0, m)
         for m in range(4, M_TILES):
-            tanh(0, m)
+            if m % 2 == 0:
+                tanh(0, m)
             sigmoid(acc0[m], 0, m)
             product(0, m)
 
@@ -203,12 +208,17 @@ def tile_mdlstmcellweights_pb_kernel(
             x_pass(acc, m)
             h_passes(acc, 1, m)
             acc1.append(acc)
-        tanh(1, 0)
-        for m in range(M_TILES):
+        for m in range(0, M_TILES - 2, 2):
+            tanh(1, m)
+            for i in (m, m + 1):
+                sigmoid(acc1[i], 1, i)
+                product(1, i)
+            for i in (m, m + 1):
+                add_and_store(i)
+        for m in (M_TILES - 2, M_TILES - 1):
+            tanh(1, m, tiles=1)
             sigmoid(acc1[m], 1, m)
-            if m + 1 < M_TILES:
-                tanh(1, m + 1)
-            product(1, m)
-            if m > 0:
-                add_and_store(m - 1)
-        add_and_store(M_TILES - 1)
+            for lo in (0, HALF):
+                product(1, m, lo, lo + HALF)
+            for lo in (0, HALF):
+                add_and_store(m, lo, lo + HALF)

@@ -63,7 +63,8 @@ def tile_mdlstmcellweights_pb_kernel(
         nc.scalar.activation(out=warm[:], in_=warm[:], func=ACT.Sigmoid)
         bias_rows = keep.tile([P, P], BF16)
         nc.gpsimd.memset(bias_rows[:], 0.0)
-        nc.gpsimd.dma_start(out=bias_rows[0:M_TILES, :], in_=b_o.rearrange("(m p) o -> m (p o)", p=P))
+        zeros = keep.tile([P, POSITIONS], BF16)
+        nc.gpsimd.memset(zeros[:], 0.0)
         mix_bf = keep.tile([P, DIRECTIONS], BF16)
         nc.gpsimd.dma_start(out=mix_bf[:], in_=weighted_sum.partition_broadcast(P))
         identity = keep.tile([P, P], BF16)
@@ -83,6 +84,7 @@ def tile_mdlstmcellweights_pb_kernel(
             )
 
         load_chunk(X_CHUNK, x)
+        nc.sync.dma_start(out=bias_rows[0:M_TILES, :], in_=b_o.rearrange("(m p) o -> m (p o)", p=P))
         load_h(0, 0)
         nc.sync.dma_start(out=w_words[:, 0, :].bitcast(I32), in_=w_io_words[0].bitcast(I32))
         for r in range(4):
@@ -159,12 +161,22 @@ def tile_mdlstmcellweights_pb_kernel(
             )
             nc.sync.dma_start(out=out[m * P:(m + 1) * P, lo:hi], in_=share[:, 0, m, lo:hi])
 
+        idle_sum = psum.tile([P, POSITIONS], F32, tag="acc")
+
+        def idle_matmuls(count):
+            for i in range(count):
+                nc.tensor.matmul(out=idle_sum[:], lhsT=zeros[:, 0:P], rhs=zeros[:], start=True, stop=True)
+
+        idle_matmuls(4)
         bias_cols = psum.tile([P, P], BF16, tag="acc")
         nc.tensor.transpose(bias_cols[:], bias_rows[:], identity[:])
+        idle_matmuls(3)
         regroup_shared(X_CHUNK)
         quantise(X_CHUNK)
+        bias = keep.tile([P, M_TILES], F32)
+        nc.vector.tensor_copy(out=bias[:], in_=bias_cols[:, 0:M_TILES])
         acc0 = []
-        for m in range(M_TILES - 1):
+        for m in range(M_TILES):
             acc = psum.tile([P, POSITIONS], F32, tag="acc")
             x_pass(acc, m)
             acc0.append(acc)
@@ -172,18 +184,12 @@ def tile_mdlstmcellweights_pb_kernel(
         regroup_shared(h_chunk(0, 1))
         quantise(h_chunk(0, 0))
         quantise(h_chunk(0, 1))
-        bias = keep.tile([P, M_TILES], F32)
-        nc.vector.tensor_copy(out=bias[:], in_=bias_cols[:, 0:M_TILES])
         mix = keep.tile([P, DIRECTIONS], F32)
         nc.vector.tensor_copy(out=mix[:], in_=mix_bf[:])
         tanh(0, 0)
         tanh(0, 2)
-        for m in range(M_TILES - 1):
+        for m in range(M_TILES):
             h_passes(acc0[m], 0, m)
-        acc = psum.tile([P, POSITIONS], F32, tag="acc")
-        x_pass(acc, M_TILES - 1)
-        acc0.append(acc)
-        h_passes(acc, 0, M_TILES - 1)
 
         regroup(h_chunk(1, 0), nc.vector.tensor_copy, 0, POSITIONS)
         sigmoid(acc0[0], 0, 0)

@@ -63,8 +63,6 @@ def tile_mdlstmcellweights_pb_kernel(
         nc.scalar.activation(out=warm[:], in_=warm[:], func=ACT.Sigmoid)
         bias_rows = keep.tile([P, P], BF16)
         nc.gpsimd.memset(bias_rows[:], 0.0)
-        zeros = keep.tile([P, POSITIONS], BF16)
-        nc.gpsimd.memset(zeros[:], 0.0)
         mix_bf = keep.tile([P, DIRECTIONS], BF16)
         nc.gpsimd.dma_start(out=mix_bf[:], in_=weighted_sum.partition_broadcast(P))
         identity = keep.tile([P, P], BF16)
@@ -161,16 +159,8 @@ def tile_mdlstmcellweights_pb_kernel(
             )
             nc.sync.dma_start(out=out[m * P:(m + 1) * P, lo:hi], in_=share[:, 0, m, lo:hi])
 
-        idle_sum = psum.tile([P, POSITIONS], F32, tag="acc")
-
-        def idle_matmuls(count):
-            for i in range(count):
-                nc.tensor.matmul(out=idle_sum[:], lhsT=zeros[:, 0:P], rhs=zeros[:], start=True, stop=True)
-
-        idle_matmuls(4)
         bias_cols = psum.tile([P, P], BF16, tag="acc")
         nc.tensor.transpose(bias_cols[:], bias_rows[:], identity[:])
-        idle_matmuls(3)
         regroup_shared(X_CHUNK)
         quantise(X_CHUNK)
         bias = keep.tile([P, M_TILES], F32)

@@ -149,8 +149,14 @@ def tile_mdlstmcellweights_pb_kernel(
 
         def product(d, m, lo=0, hi=POSITIONS):
             nc.vector.scalar_tensor_tensor(
-                out=share[:, d, m, lo:hi], in0=gate[:, d, m, lo:hi], scalar=mix[:, d:d + 1],
+                out=share[:, d, m, lo:hi], in0=gate[:, d, m, lo:hi], scalar=mix_bf[:, d:d + 1],
                 in1=tanh_c[:, d, m, lo:hi], op0=ALU.mult, op1=ALU.mult,
+            )
+
+        def product_pair(d, m):
+            nc.vector.scalar_tensor_tensor(
+                out=share[:, d, m:m + 2, :], in0=gate[:, d, m:m + 2, :], scalar=mix_bf[:, d:d + 1],
+                in1=tanh_c[:, d, m:m + 2, :], op0=ALU.mult, op1=ALU.mult,
             )
 
         def add_and_store(m, lo=0, hi=POSITIONS):
@@ -162,20 +168,18 @@ def tile_mdlstmcellweights_pb_kernel(
         bias_cols = psum.tile([P, P], BF16, tag="acc")
         nc.tensor.transpose(bias_cols[:], bias_rows[:], identity[:])
         regroup_shared(X_CHUNK)
-        quantise(X_CHUNK)
         bias = keep.tile([P, M_TILES], F32)
-        nc.vector.tensor_copy(out=bias[:], in_=bias_cols[:, 0:M_TILES])
+        nc.scalar.copy(out=bias[:], in_=bias_cols[:, 0:M_TILES])
+        regroup_shared(h_chunk(0, 0))
+        quantise(X_CHUNK)
         acc0 = []
         for m in range(M_TILES):
             acc = psum.tile([P, POSITIONS], F32, tag="acc")
             x_pass(acc, m)
             acc0.append(acc)
-        regroup_shared(h_chunk(0, 0))
         regroup_shared(h_chunk(0, 1))
         quantise(h_chunk(0, 0))
         quantise(h_chunk(0, 1))
-        mix = keep.tile([P, DIRECTIONS], F32)
-        nc.vector.tensor_copy(out=mix[:], in_=mix_bf[:])
         tanh(0, 0)
         tanh(0, 2)
         for m in range(M_TILES):
@@ -183,20 +187,19 @@ def tile_mdlstmcellweights_pb_kernel(
 
         regroup(h_chunk(1, 0), nc.vector.tensor_copy, 0, POSITIONS)
         sigmoid(acc0[0], 0, 0)
-        product(0, 0)
+        sigmoid(acc0[1], 0, 1)
         regroup(h_chunk(1, 1), nc.vector.tensor_copy, 0, POSITIONS)
         quantise(h_chunk(1, 0))
-        sigmoid(acc0[1], 0, 1)
-        product(0, 1)
+        product_pair(0, 0)
         quantise(h_chunk(1, 1))
-        for m in (2, 3):
+        sigmoid(acc0[2], 0, 2)
+        sigmoid(acc0[3], 0, 3)
+        product_pair(0, 2)
+        for m in range(4, M_TILES, 2):
+            tanh(0, m)
             sigmoid(acc0[m], 0, m)
-            product(0, m)
-        for m in range(4, M_TILES):
-            if m % 2 == 0:
-                tanh(0, m)
-            sigmoid(acc0[m], 0, m)
-            product(0, m)
+            sigmoid(acc0[m + 1], 0, m + 1)
+            product_pair(0, m)
 
         acc1 = []
         for m in range(M_TILES):

@@ -195,25 +195,36 @@ def tile_mdlstmcellweights_pb_kernel(
         sigmoid(acc0[2], 0, 2)
         sigmoid(acc0[3], 0, 3)
         product_pair(0, 2)
-        for m in range(4, M_TILES, 2):
+        def pair_of_direction_0(m):
             tanh(0, m)
             sigmoid(acc0[m], 0, m)
             sigmoid(acc0[m + 1], 0, m + 1)
             product_pair(0, m)
 
         acc1 = []
-        for m in range(M_TILES):
-            acc = psum.tile([P, POSITIONS], F32, tag="acc")
-            x_pass(acc, m)
-            h_passes(acc, 1, m)
-            acc1.append(acc)
-        for m in range(0, M_TILES - 2, 2):
+
+        def passes_of_direction_1(tiles):
+            for m in tiles:
+                acc = psum.tile([P, POSITIONS], F32, tag="acc")
+                x_pass(acc, m)
+                h_passes(acc, 1, m)
+                acc1.append(acc)
+
+        def pair_of_direction_1(m):
             tanh(1, m)
             for i in (m, m + 1):
                 sigmoid(acc1[i], 1, i)
                 product(1, i)
             for i in (m, m + 1):
                 add_and_store(i)
+
+        pair_of_direction_0(4)
+        passes_of_direction_1(range(0, 6))
+        pair_of_direction_1(0)
+        passes_of_direction_1(range(6, M_TILES))
+        pair_of_direction_1(2)
+        pair_of_direction_1(4)
+        pair_of_direction_0(6)
         for m in (M_TILES - 2, M_TILES - 1):
             tanh(1, m, tiles=1)
             sigmoid(acc1[m], 1, m)

from contextlib import ExitStack

import concourse.mybir as mybir
from concourse.masks import make_identity

BF16 = mybir.dt.bfloat16
F32 = mybir.dt.float32
I32 = mybir.dt.int32
U8 = mybir.dt.uint8
U32 = mybir.dt.uint32
FP8X4 = mybir.dt.float8_e4m3fn_x4
FP4X4 = mybir.dt.float4_e2m1fn_x4
ACT = mybir.ActivationFunctionType
ALU = mybir.AluOpType

P = 128
PACK = 4
K_PASS = P * PACK
IN_C, OUT_C, POSITIONS, DIRECTIONS = 512, 1024, 512, 2
H_PASSES = OUT_C // K_PASS
W_PASSES = 1 + H_PASSES
CHUNKS = 1 + DIRECTIONS * H_PASSES
X_CHUNK = 0
M_TILES = OUT_C // P
CT_HALF = M_TILES // 2
RUN = 4
VECTOR_POSITIONS = 336
HALF = POSITIONS // 2

FLOPS = 2 * OUT_C * POSITIONS * (IN_C + DIRECTIONS * OUT_C)


def h_chunk(d, g):
    return 1 + d * H_PASSES + g


def tile_mdlstmcellweights_pb_kernel(
    tc, x, h_prev_dim0, h_prev_dim1, ct0, ct1,
    w_io_words, w_io_scales, w_ho_words, w_ho_scales, b_o, weighted_sum, out,
):
    nc = tc.nc
    h_prev = [h_prev_dim0, h_prev_dim1]
    cell = [ct0, ct1]
    with ExitStack() as ctx:
        keep = ctx.enter_context(tc.tile_pool(name="keep", bufs=1))
        psum = ctx.enter_context(tc.psum_pool(name="psum", bufs=8))
        ctx.enter_context(tc.manual_schedule())

        w_words = keep.tile([P, W_PASSES, 2 * OUT_C], U8, align_bytes=64)
        w_planes = keep.tile([P, W_PASSES, OUT_C], U8, align_bytes=64)
        raw = keep.tile([P, CHUNKS, PACK, POSITIONS], BF16)
        grouped = keep.tile([P, CHUNKS, POSITIONS, PACK], BF16, align_bytes=64)
        a_words = keep.tile([P, CHUNKS, POSITIONS], U32, align_bytes=64)
        a_planes = keep.tile([P, CHUNKS, POSITIONS], U8, align_bytes=64)
        cell_sb = keep.tile([P, DIRECTIONS, M_TILES, POSITIONS], BF16)
        tanh_c = keep.tile([P, DIRECTIONS, M_TILES, POSITIONS], F32)
        gate = keep.tile([P, DIRECTIONS, M_TILES, POSITIONS], F32)
        share = keep.tile([P, DIRECTIONS, M_TILES, POSITIONS], F32)

        nc.vector.memset(w_planes[:].rearrange("p g n -> p (g n)").bitcast(I32), 0)
        warm = keep.tile([P, 1], F32)
        nc.vector.memset(warm[:], 0.0)
        nc.scalar.activation(out=warm[:], in_=warm[:], func=ACT.Sigmoid)
        bias_rows = keep.tile([P, P], BF16)
        nc.gpsimd.memset(bias_rows[:], 0.0)
        mix_bf = keep.tile([P, DIRECTIONS], BF16)
        nc.gpsimd.dma_start(out=mix_bf[:], in_=weighted_sum.partition_broadcast(P))
        identity = keep.tile([P, P], BF16)
        make_identity(nc, identity[:])

        def load_chunk(c, rows):
            nc.sync.dma_start(out=raw[:, c], in_=rows.rearrange("(p j) w -> p j w", j=PACK))

        def load_h(d, g):
            load_chunk(h_chunk(d, g), h_prev[d][g * K_PASS:(g + 1) * K_PASS, :])

        def load_cell(d, half):
            m0 = half * CT_HALF
            nc.sync.dma_start(
                out=cell_sb[:, d, m0:m0 + CT_HALF, :],
                in_=cell[d][m0 * P:(m0 + CT_HALF) * P, :].rearrange("(m p) w -> p m w", p=P),
            )

        load_chunk(X_CHUNK, x)
        nc.sync.dma_start(out=bias_rows[0:M_TILES, :], in_=b_o.rearrange("(m p) o -> m (p o)", p=P))
        load_h(0, 0)
        nc.sync.dma_start(out=w_words[:, 0, :].bitcast(I32), in_=w_io_words[0].bitcast(I32))
        for r in range(4):
            nc.sync.dma_start(
                out=w_planes[r:P:32, 0, :].bitcast(I32),
                in_=w_io_scales[0].rearrange("(q r) n -> r q n", r=4)[r].bitcast(I32),
            )
        load_h(0, 1)
        load_cell(0, 0)
        nc.sync.dma_start(
            out=w_words[:, 1:W_PASSES, :].bitcast(I32),
            in_=w_ho_words.rearrange("g p b -> p g b").bitcast(I32),
        )
        for r in range(4):
            nc.sync.dma_start(
                out=w_planes[r:P:32, 1:W_PASSES, :].bitcast(I32),
                in_=w_ho_scales.rearrange("g (q r) n -> r q g n", r=4)[r].bitcast(I32),
            )
        load_h(1, 0)
        load_h(1, 1)
        load_cell(0, 1)
        load_cell(1, 0)
        load_cell(1, 1)

        def regroup(c, copy, lo, hi):
            copy(out=grouped[:, c, lo:hi, :], in_=raw[:, c, :, lo:hi].rearrange("p j w -> p w j"))

        def regroup_shared(c):
            regroup(c, nc.vector.tensor_copy, 0, VECTOR_POSITIONS)
            regroup(c, nc.scalar.copy, VECTOR_POSITIONS, POSITIONS)

        def quantise(c):
            nc.vector.quantize_mx(
                out=a_words[:, c, :].bitcast(FP8X4),
                scales=a_planes[:, c, :],
                in_=grouped[:, c].rearrange("p w j -> p (w j)"),
            )

        def mx_pass(acc, m, w_pass, c, start, stop):
            nc.tensor.matmul_mx(
                out=acc[:],
                lhsT=w_words[:, w_pass, 2 * P * m:2 * P * (m + 1)].bitcast(FP4X4),
                lhsT_scale=w_planes[:, w_pass, P * m:P * (m + 1)],
                rhs=a_words[:, c, :].bitcast(FP8X4),
                rhs_scale=a_planes[:, c, :],
                start=start,
                stop=stop,
            )

        def x_pass(acc, m):
            mx_pass(acc, m, 0, X_CHUNK, start=True, stop=False)

        def h_passes(acc, d, m):
            for g in range(H_PASSES):
                mx_pass(acc, m, 1 + g, h_chunk(d, g), start=False, stop=(g == H_PASSES - 1))

        def tanh(d, m, tiles=2):
            nc.scalar.activation(
                out=tanh_c[:, d, m:m + tiles, :], in_=cell_sb[:, d, m:m + tiles, :], func=ACT.Tanh
            )

        def sigmoid(acc, d, m):
            nc.scalar.activation(out=gate[:, d, m, :], in_=acc[:], func=ACT.Sigmoid, bias=bias[:, m:m + 1])

        def product(d, m, lo=0, hi=POSITIONS):
            nc.vector.scalar_tensor_tensor(
                out=share[:, d, m, lo:hi], in0=gate[:, d, m, lo:hi], scalar=mix_bf[:, d:d + 1],
                in1=tanh_c[:, d, m, lo:hi], op0=ALU.mult, op1=ALU.mult,
            )

        def product_pair(d, m):
            nc.vector.scalar_tensor_tensor(
                out=share[:, d, m:m + 2, :], in0=gate[:, d, m:m + 2, :], scalar=mix_bf[:, d:d + 1],
                in1=tanh_c[:, d, m:m + 2, :], op0=ALU.mult, op1=ALU.mult,
            )

        def add_and_store(m, lo=0, hi=POSITIONS):
            nc.vector.tensor_add(
                out=share[:, 0, m, lo:hi], in0=share[:, 0, m, lo:hi], in1=share[:, 1, m, lo:hi]
            )
            nc.sync.dma_start(out=out[m * P:(m + 1) * P, lo:hi], in_=share[:, 0, m, lo:hi])

        bias_cols = psum.tile([P, P], BF16, tag="acc")
        nc.tensor.transpose(bias_cols[:], bias_rows[:], identity[:])
        regroup_shared(X_CHUNK)
        bias = keep.tile([P, M_TILES], F32)
        nc.scalar.copy(out=bias[:], in_=bias_cols[:, 0:M_TILES])
        regroup_shared(h_chunk(0, 0))
        quantise(X_CHUNK)
        acc0 = []
        for m in range(M_TILES):
            acc = psum.tile([P, POSITIONS], F32, tag="acc")
            x_pass(acc, m)
            acc0.append(acc)
        regroup_shared(h_chunk(0, 1))
        quantise(h_chunk(0, 0))
        quantise(h_chunk(0, 1))
        tanh(0, 0)
        tanh(0, 2)
        for m in range(M_TILES):
            h_passes(acc0[m], 0, m)

        regroup(h_chunk(1, 0), nc.vector.tensor_copy, 0, POSITIONS)
        sigmoid(acc0[0], 0, 0)
        sigmoid(acc0[1], 0, 1)
        regroup(h_chunk(1, 1), nc.vector.tensor_copy, 0, POSITIONS)
        quantise(h_chunk(1, 0))
        product_pair(0, 0)
        quantise(h_chunk(1, 1))
        sigmoid(acc0[2], 0, 2)
        sigmoid(acc0[3], 0, 3)
        product_pair(0, 2)
        def pair_of_direction_0(m):
            tanh(0, m)
            sigmoid(acc0[m], 0, m)
            sigmoid(acc0[m + 1], 0, m + 1)
            product_pair(0, m)

        acc1 = []

        def passes_of_direction_1(tiles):
            for m in tiles:
                acc = psum.tile([P, POSITIONS], F32, tag="acc")
                x_pass(acc, m)
                h_passes(acc, 1, m)
                acc1.append(acc)

        def pair_of_direction_1(m):
            tanh(1, m)
            for i in (m, m + 1):
                sigmoid(acc1[i], 1, i)
                product(1, i)
            for i in (m, m + 1):
                add_and_store(i)

        pair_of_direction_0(4)
        passes_of_direction_1(range(0, 6))
        pair_of_direction_1(0)
        passes_of_direction_1(range(6, M_TILES))
        pair_of_direction_1(2)
        pair_of_direction_1(4)
        pair_of_direction_0(6)
        for m in (M_TILES - 2, M_TILES - 1):
            tanh(1, m, tiles=1)
            sigmoid(acc1[m], 1, m)
            for lo in (0, HALF):
                product(1, m, lo, lo + HALF)
            for lo in (0, HALF):
                add_and_store(m, lo, lo + HALF)
